import numpy as np
import ml_dtypes


def mxq(x, axis, fmt="e4m3"):
    dtype, down = {"e4m3": (ml_dtypes.float8_e4m3fn, 7), "e5m2": (ml_dtypes.float8_e5m2, 14)}[fmt]
    v = np.moveaxis(np.asarray(x, np.float32).astype(ml_dtypes.bfloat16).astype(np.float64), axis, -1)
    blocks = v.reshape(v.shape[:-1] + (-1, 32))
    amax = np.abs(blocks).max(-1, keepdims=True)
    byte = np.maximum(np.where(amax > 0, np.frexp(amax)[1] - 1 + 127, 0) - down, 1)
    scale = np.exp2(byte - 127.0)
    codes = (blocks / scale).astype(np.float32).astype(dtype).astype(np.float64)
    return np.moveaxis((codes * scale).reshape(v.shape), -1, axis)


WIDE = False


def mx_kscale(k):
    if not WIDE:
        return np.ones(k)
    levels = np.array([10, -10, 5, -5, 0])
    a = np.random.permutation(np.resize(levels, k // 512 * 4)).reshape(k // 512, 4)
    idx = np.arange(k)
    return np.exp2(a[idx // 512, idx % 128 // 32])


BF16 = ml_dtypes.bfloat16


def bf(x):
    return np.asarray(x, np.float32).astype(BF16)


def f64(x):
    return np.asarray(x).astype(np.float64)


B, S, D, E, R = 4, 2048, 1024, 8, 32


def setup_inputs():
    s = mx_kscale(D)
    return {"x": bf(np.random.standard_normal((B, S, D)) * s),
            "W": bf(np.random.standard_normal((E, R, D)) * (1.0 / np.sqrt(D)) / s)}


def reference(x, W):
    xq = mxq(f64(x), 2, "e4m3")
    Wq = mxq(f64(W), 2, "e4m3")
    y = xq[None, :, :, :] @ Wq.transpose(0, 2, 1)[:, None, :, :]
    return tuple(y[e] for e in range(W.shape[0]))

@@ -1,0 +1,195 @@
+from contextlib import ExitStack
+
+import concourse.mybir as mybir
+from concourse.masks import make_identity
+
+F32 = mybir.dt.float32
+BF16 = mybir.dt.bfloat16
+U32 = mybir.dt.uint32
+U8 = mybir.dt.uint8
+FP8X4 = mybir.dt.float8_e4m3fn_x4
+
+P = 128
+D = 1024
+ROWS = 8192
+E = 8
+R = 32
+COLS = E * R
+NT = ROWS // P
+QUAD = 4
+NQ = NT // QUAD
+WORDS = D // 2
+
+FLOPS = 2 * ROWS * D * COLS
+
+GROUPS = (32, 16, 8, 8)
+CHUNKS = (1, 1, 2, 4, 8, 8, 8, 8, 8, 8, 8)
+BIG = 8
+BIG_BUFS = 5
+MANUAL = True
+
+
+def tile_moelineara_t_kernel(tc, x, W, *outs):
+    nc = tc.nc
+    xf = x.flatten_outer_dims()
+    wf = W.flatten_outer_dims()
+    of = [o.flatten_outer_dims() for o in outs]
+
+    group_of = []
+    first = 0
+    for s, t_count in enumerate(GROUPS):
+        for k in range(t_count):
+            group_of.append((s, first, t_count))
+        first += t_count
+    chunk_first = []
+    first = 0
+    for cnt in CHUNKS:
+        chunk_first.append(first)
+        first += cnt
+    assert first == NT
+
+    with ExitStack() as ctx:
+        const = ctx.enter_context(tc.tile_pool(name="const", bufs=1))
+        xpool = ctx.enter_context(tc.tile_pool(name="xpool", bufs=1))
+        gpool = ctx.enter_context(tc.tile_pool(name="gpool", bufs=3))
+        opool = ctx.enter_context(tc.tile_pool(name="opool", bufs=1))
+        psum_t = ctx.enter_context(tc.psum_pool(name="psum_t", bufs=5))
+        psum_o = ctx.enter_context(tc.psum_pool(name="psum_o", bufs=3))
+        if MANUAL:
+            ctx.enter_context(tc.manual_schedule())
+
+        tile_src = {}
+
+        def load_chunk(c):
+            cnt = CHUNKS[c]
+            n0 = chunk_first[c]
+            s, g0, t_count = group_of[n0]
+            if cnt == BIG:
+                xc = xpool.tile([P, cnt * D], BF16, name="xbig", tag="xbig", bufs=BIG_BUFS)
+            else:
+                xc = xpool.tile([P, cnt * D], BF16, name="xs%d" % c, tag="xs%d" % c)
+            rows = xf[g0 * P:(g0 + t_count) * P, :].rearrange("(p t) k -> p t k", t=t_count)
+            nc.sync.dma_start(
+                out=xc[:].rearrange("p (t k) -> p t k", k=D),
+                in_=rows[:, n0 - g0:n0 - g0 + cnt, :],
+            )
+            xw = xc[:].bitcast(F32)
+            for j in range(cnt):
+                tile_src[n0 + j] = (xw, j * WORDS)
+
+        w_raw = const.tile([P, 2 * D], BF16, name="w_raw")
+        nc.sync.dma_start(
+            out=w_raw[:].rearrange("p (h k) -> p h k", h=2),
+            in_=wf.rearrange("(h p) k -> p h k", p=P),
+        )
+        n_first = sum(1 for cnt in CHUNKS if cnt != BIG) + BIG_BUFS
+        n_first = min(n_first, len(CHUNKS))
+        for c in range(n_first):
+            load_chunk(c)
+        next_chunk = [n_first]
+
+        ident = const.tile([P, P], F32, name="ident")
+        make_identity(nc, ident[:])
+
+        w_grouped = const.tile([P, 2 * COLS * 4], BF16, name="w_grouped", align_bytes=64)
+        w_words = const.tile([P, 2 * COLS], U32, name="w_words", align_bytes=64)
+        w_scales = const.tile([P, 2 * COLS], U8, name="w_scales", align_bytes=64)
+        ww = w_raw[:].bitcast(F32)
+        wg = w_grouped[:].bitcast(F32).rearrange("p (g c u) -> p g c u", g=2, u=2)
+        for h in range(2):
+            xt = psum_t.tile([P, 512], F32, name="xt")
+            for b in range(4):
+                nc.tensor.transpose(
+                    xt[:, b * P:(b + 1) * P],
+                    ww[:, h * WORDS + b * P:h * WORDS + (b + 1) * P],
+                    ident[:],
+                )
+            src = xt[:].rearrange("p (g u r) -> p g r u", g=2, u=2)
+            if h == 0:
+                nc.vector.tensor_copy(out=wg[:, :, h * P:(h + 1) * P, :], in_=src)
+            else:
+                nc.scalar.copy(out=wg[:, :, h * P:(h + 1) * P, :], in_=src)
+        nc.vector.quantize_mx(out=w_words[:].bitcast(FP8X4), scales=w_scales[:], in_=w_grouped[:])
+
+        grouped = {}
+        quant = {}
+        accs = {}
+        out_sb = {}
+
+        def transpose_quad(q):
+            gt = gpool.tile([P, QUAD * D], BF16, name="grouped", align_bytes=64)
+            grouped[q] = gt
+            gf = gt[:].bitcast(F32)
+            for j in range(QUAD):
+                xw, off = tile_src[QUAD * q + j]
+                xt = psum_t.tile([P, 512], F32, name="xt")
+                for b in range(4):
+                    nc.tensor.transpose(
+                        xt[:, b * P:(b + 1) * P],
+                        xw[:, off + b * P:off + (b + 1) * P],
+                        ident[:],
+                    )
+                nc.scalar.copy(
+                    out=gf[:, j * WORDS:(j + 1) * WORDS].rearrange("p (g r u) -> p g r u", g=2, u=2),
+                    in_=xt[:].rearrange("p (g u r) -> p g r u", g=2, u=2),
+                )
+
+        def quantise_quad(q):
+            words = gpool.tile([P, QUAD * 2 * P], U32, name="words", align_bytes=64)
+            scales = gpool.tile([P, QUAD * 2 * P], U8, name="scales", align_bytes=64)
+            nc.vector.quantize_mx(out=words[:].bitcast(FP8X4), scales=scales[:], in_=grouped[q][:])
+            quant[q] = (words, scales)
+
+        def mx_quad(q):
+            words, scales = quant[q]
+            accs[q] = []
+            for h in range(2):
+                acc = psum_o.tile([P, 512], F32, name="acc")
+                for jj in range(2):
+                    for g in range(2):
+                        c0 = ((2 * h + jj) * 2 + g) * P
+                        nc.tensor.matmul_mx(
+                            out=acc[:, jj * COLS:(jj + 1) * COLS],
+                            lhsT=words[:, c0:c0 + P].bitcast(FP8X4),
+                            lhsT_scale=scales[:, c0:c0 + P],
+                            rhs=w_words[:, g * COLS:(g + 1) * COLS].bitcast(FP8X4),
+                            rhs_scale=w_scales[:, g * COLS:(g + 1) * COLS],
+                            start=(g == 0),
+                            stop=(g == 1),
+                        )
+                accs[q].append(acc)
+
+        def out_quad(q):
+            n0 = QUAD * q
+            s, g0, t_count = group_of[n0]
+            if n0 == g0:
+                out_sb[s] = opool.tile([P, E * t_count * R], F32, name="out%d" % s, tag="out%d" % s)
+            ov = out_sb[s][:].rearrange("p (e t r) -> p e t r", e=E, r=R)
+            for h in range(2):
+                t0 = n0 - g0 + 2 * h
+                nc.vector.tensor_copy(
+                    out=ov[:, :, t0:t0 + 2, :],
+                    in_=accs[q][h][:].rearrange("p (t e r) -> p e t r", t=2, r=R),
+                )
+            if n0 + QUAD == g0 + t_count:
+                for e in range(E):
+                    nc.sync.dma_start(
+                        out=of[e][g0 * P:(g0 + t_count) * P, :].rearrange("(p t) r -> p t r", t=t_count),
+                        in_=ov[:, e, :, :],
+                    )
+
+        for i in range(NQ + 3):
+            if i < NQ:
+                transpose_quad(i)
+                c = next_chunk[0]
+                if c < len(CHUNKS):
+                    old = c - BIG_BUFS
+                    if chunk_first[old] + CHUNKS[old] == QUAD * (i + 1):
+                        load_chunk(c)
+                        next_chunk[0] = c + 1
+            if 0 <= i - 3 < NQ:
+                out_quad(i - 3)
+            if 0 <= i - 1 < NQ:
+                quantise_quad(i - 1)
+            if 0 <= i - 2 < NQ:
+                mx_quad(i - 2)

@@ -16,17 +16,15 @@ E = 8
 R = 32
 COLS = E * R
 NT = ROWS // P
-QUAD = 4
-NQ = NT // QUAD
 WORDS = D // 2
+UNIT = 4
 
 FLOPS = 2 * ROWS * D * COLS
 
-GROUPS = (32, 16, 8, 8)
-CHUNKS = (1, 1, 2, 4, 8, 8, 8, 8, 8, 8, 8)
-BIG = 8
-BIG_BUFS = 5
-MANUAL = True
+GROUPS = (32, 24, 8)
+CHUNKS = (1, 1, 2, 4, 4, 4, 4, 4, 4, 4, 8, 8, 8, 4, 4)
+CHUNK_BUFS = {1: 2, 2: 1, 4: 5, 8: 3}
+RUNS = (2, 2, 4, 8, 8, 8, 8, 8, 8, 4, 2, 2)
 
 
 def tile_moelineara_t_kernel(tc, x, W, *outs):
@@ -38,13 +36,19 @@ def tile_moelineara_t_kernel(tc, x, W, *outs):
     group_of = []
     first = 0
     for s, t_count in enumerate(GROUPS):
-        for k in range(t_count):
-            group_of.append((s, first, t_count))
+        group_of.extend([(s, first, t_count)] * t_count)
         first += t_count
+    assert first == NT
     chunk_first = []
     first = 0
     for cnt in CHUNKS:
         chunk_first.append(first)
+        first += cnt
+    assert first == NT
+    run_first = []
+    first = 0
+    for cnt in RUNS:
+        run_first.append(first)
         first += cnt
     assert first == NT
 
@@ -52,41 +56,61 @@ def tile_moelineara_t_kernel(tc, x, W, *outs):
         const = ctx.enter_context(tc.tile_pool(name="const", bufs=1))
         xpool = ctx.enter_context(tc.tile_pool(name="xpool", bufs=1))
         gpool = ctx.enter_context(tc.tile_pool(name="gpool", bufs=3))
+        qpool = ctx.enter_context(tc.tile_pool(name="qpool", bufs=4))
         opool = ctx.enter_context(tc.tile_pool(name="opool", bufs=1))
-        psum_t = ctx.enter_context(tc.psum_pool(name="psum_t", bufs=5))
-        psum_o = ctx.enter_context(tc.psum_pool(name="psum_o", bufs=3))
-        if MANUAL:
-            ctx.enter_context(tc.manual_schedule())
+        psum_t = ctx.enter_context(tc.psum_pool(name="psum_t", bufs=4))
+        psum_o = ctx.enter_context(tc.psum_pool(name="psum_o", bufs=4))
+        ctx.enter_context(tc.manual_schedule())
 
         tile_src = {}
+        holders = {}
+        state = {"chunk": 0, "transposed": 0}
 
-        def load_chunk(c):
-            cnt = CHUNKS[c]
-            n0 = chunk_first[c]
-            s, g0, t_count = group_of[n0]
-            if cnt == BIG:
-                xc = xpool.tile([P, cnt * D], BF16, name="xbig", tag="xbig", bufs=BIG_BUFS)
+        def load_chunks():
+            while state["chunk"] < len(CHUNKS):
+                c = state["chunk"]
+                cnt = CHUNKS[c]
+                held = holders.get(cnt, [])
+                if len(held) >= CHUNK_BUFS[cnt]:
+                    old = held[len(held) - CHUNK_BUFS[cnt]]
+                    if chunk_first[old] + cnt > state["transposed"]:
+                        return
+                holders[cnt] = held + [c]
+                state["chunk"] = c + 1
+                n0 = chunk_first[c]
+                s, g0, t_count = group_of[n0]
+                xc = xpool.tile([P, cnt * D], BF16, name="x%d" % cnt, tag="x%d" % cnt, bufs=CHUNK_BUFS[cnt])
+                rows = xf[g0 * P:(g0 + t_count) * P, :].rearrange("(p t) k -> p t k", t=t_count)
+                nc.sync.dma_start(
+                    out=xc[:].rearrange("p (t k) -> p t k", k=D),
+                    in_=rows[:, n0 - g0:n0 - g0 + cnt, :],
+                )
+                xw = xc[:].bitcast(F32)
+                for j in range(cnt):
+                    tile_src[n0 + j] = (xw, j * WORDS)
+
+        def transpose_tile(words_ap, first_word):
+            xt = psum_t.tile([P, 4 * P], F32, name="xt")
+            for b in range(4):
+                nc.tensor.transpose(
+                    xt[:, b * P:(b + 1) * P],
+                    words_ap[:, first_word + b * P:first_word + (b + 1) * P],
+                    ident[:],
+                )
+            return xt[:].rearrange("p (g u r) -> p g r u", g=2, u=2)
+
+        def copy_on(k, out, in_):
+            if k % 2 == 0:
+                nc.vector.tensor_copy(out=out, in_=in_)
             else:
-                xc = xpool.tile([P, cnt * D], BF16, name="xs%d" % c, tag="xs%d" % c)
-            rows = xf[g0 * P:(g0 + t_count) * P, :].rearrange("(p t) k -> p t k", t=t_count)
-            nc.sync.dma_start(
-                out=xc[:].rearrange("p (t k) -> p t k", k=D),
-                in_=rows[:, n0 - g0:n0 - g0 + cnt, :],
-            )
-            xw = xc[:].bitcast(F32)
-            for j in range(cnt):
-                tile_src[n0 + j] = (xw, j * WORDS)
+                nc.scalar.copy(out=out, in_=in_)
 
         w_raw = const.tile([P, 2 * D], BF16, name="w_raw")
         nc.sync.dma_start(
             out=w_raw[:].rearrange("p (h k) -> p h k", h=2),
             in_=wf.rearrange("(h p) k -> p h k", p=P),
         )
-        n_first = sum(1 for cnt in CHUNKS if cnt != BIG) + BIG_BUFS
-        n_first = min(n_first, len(CHUNKS))
-        for c in range(n_first):
-            load_chunk(c)
-        next_chunk = [n_first]
+        load_chunks()
 
         ident = const.tile([P, P], F32, name="ident")
         make_identity(nc, ident[:])
@@ -94,102 +118,70 @@ def tile_moelineara_t_kernel(tc, x, W, *outs):
         w_grouped = const.tile([P, 2 * COLS * 4], BF16, name="w_grouped", align_bytes=64)
         w_words = const.tile([P, 2 * COLS], U32, name="w_words", align_bytes=64)
         w_scales = const.tile([P, 2 * COLS], U8, name="w_scales", align_bytes=64)
-        ww = w_raw[:].bitcast(F32)
         wg = w_grouped[:].bitcast(F32).rearrange("p (g c u) -> p g c u", g=2, u=2)
         for h in range(2):
-            xt = psum_t.tile([P, 512], F32, name="xt")
-            for b in range(4):
-                nc.tensor.transpose(
-                    xt[:, b * P:(b + 1) * P],
-                    ww[:, h * WORDS + b * P:h * WORDS + (b + 1) * P],
-                    ident[:],
-                )
-            src = xt[:].rearrange("p (g u r) -> p g r u", g=2, u=2)
-            if h == 0:
-                nc.vector.tensor_copy(out=wg[:, :, h * P:(h + 1) * P, :], in_=src)
-            else:
-                nc.scalar.copy(out=wg[:, :, h * P:(h + 1) * P, :], in_=src)
+            copy_on(h, wg[:, :, h * P:(h + 1) * P, :], transpose_tile(w_raw[:].bitcast(F32), h * WORDS))
         nc.vector.quantize_mx(out=w_words[:].bitcast(FP8X4), scales=w_scales[:], in_=w_grouped[:])
 
-        grouped = {}
         quant = {}
-        accs = {}
         out_sb = {}
 
-        def transpose_quad(q):
-            gt = gpool.tile([P, QUAD * D], BF16, name="grouped", align_bytes=64)
-            grouped[q] = gt
-            gf = gt[:].bitcast(F32)
-            for j in range(QUAD):
-                xw, off = tile_src[QUAD * q + j]
-                xt = psum_t.tile([P, 512], F32, name="xt")
-                for b in range(4):
-                    nc.tensor.transpose(
-                        xt[:, b * P:(b + 1) * P],
-                        xw[:, off + b * P:off + (b + 1) * P],
-                        ident[:],
+        def transpose_run(i):
+            n0 = run_first[i]
+            units = []
+            for u0 in range(n0, n0 + RUNS[i], UNIT):
+                cnt = min(UNIT, n0 + RUNS[i] - u0)
+                gt = gpool.tile([P, cnt * D], BF16, name="grouped", align_bytes=64)
+                gf = gt[:].bitcast(F32)
+                for j in range(cnt):
+                    xw, off = tile_src[u0 + j]
+                    copy_on(
+                        u0 + j,
+                        gf[:, j * WORDS:(j + 1) * WORDS].rearrange("p (g r u) -> p g r u", g=2, u=2),
+                        transpose_tile(xw, off),
                     )
-                nc.scalar.copy(
-                    out=gf[:, j * WORDS:(j + 1) * WORDS].rearrange("p (g r u) -> p g r u", g=2, u=2),
-                    in_=xt[:].rearrange("p (g u r) -> p g r u", g=2, u=2),
-                )
+                units.append((u0, cnt, gt))
+            state["transposed"] = n0 + RUNS[i]
+            load_chunks()
+            for u0, cnt, gt in units:
+                words = qpool.tile([P, cnt * 2 * P], U32, name="words", align_bytes=64)
+                scales = qpool.tile([P, cnt * 2 * P], U8, name="scales", align_bytes=64)
+                nc.vector.quantize_mx(out=words[:].bitcast(FP8X4), scales=scales[:], in_=gt[:])
+                for j in range(cnt):
+                    quant[u0 + j] = (words, scales, j * 2 * P)
 
-        def quantise_quad(q):
-            words = gpool.tile([P, QUAD * 2 * P], U32, name="words", align_bytes=64)
-            scales = gpool.tile([P, QUAD * 2 * P], U8, name="scales", align_bytes=64)
-            nc.vector.quantize_mx(out=words[:].bitcast(FP8X4), scales=scales[:], in_=grouped[q][:])
-            quant[q] = (words, scales)
-
-        def mx_quad(q):
-            words, scales = quant[q]
-            accs[q] = []
-            for h in range(2):
-                acc = psum_o.tile([P, 512], F32, name="acc")
+        def multiply_run(i):
+            for n in range(run_first[i], run_first[i] + RUNS[i], 2):
+                acc = psum_o.tile([P, 2 * COLS], F32, name="acc")
                 for jj in range(2):
+                    words, scales, c0 = quant[n + jj]
                     for g in range(2):
-                        c0 = ((2 * h + jj) * 2 + g) * P
                         nc.tensor.matmul_mx(
                             out=acc[:, jj * COLS:(jj + 1) * COLS],
-                            lhsT=words[:, c0:c0 + P].bitcast(FP8X4),
-                            lhsT_scale=scales[:, c0:c0 + P],
+                            lhsT=words[:, c0 + g * P:c0 + (g + 1) * P].bitcast(FP8X4),
+                            lhsT_scale=scales[:, c0 + g * P:c0 + (g + 1) * P],
                             rhs=w_words[:, g * COLS:(g + 1) * COLS].bitcast(FP8X4),
                             rhs_scale=w_scales[:, g * COLS:(g + 1) * COLS],
                             start=(g == 0),
                             stop=(g == 1),
                         )
-                accs[q].append(acc)
-
-        def out_quad(q):
-            n0 = QUAD * q
-            s, g0, t_count = group_of[n0]
-            if n0 == g0:
-                out_sb[s] = opool.tile([P, E * t_count * R], F32, name="out%d" % s, tag="out%d" % s)
-            ov = out_sb[s][:].rearrange("p (e t r) -> p e t r", e=E, r=R)
-            for h in range(2):
-                t0 = n0 - g0 + 2 * h
-                nc.vector.tensor_copy(
-                    out=ov[:, :, t0:t0 + 2, :],
-                    in_=accs[q][h][:].rearrange("p (t e r) -> p e t r", t=2, r=R),
+                s, g0, t_count = group_of[n]
+                if n == g0:
+                    out_sb[s] = opool.tile([P, E * t_count * R], F32, name="out%d" % s, tag="out%d" % s)
+                ov = out_sb[s][:].rearrange("p (e t r) -> p e t r", e=E, r=R)
+                nc.scalar.copy(
+                    out=ov[:, :, n - g0:n - g0 + 2, :],
+                    in_=acc[:].rearrange("p (t e r) -> p e t r", t=2, r=R),
                 )
-            if n0 + QUAD == g0 + t_count:
-                for e in range(E):
-                    nc.sync.dma_start(
-                        out=of[e][g0 * P:(g0 + t_count) * P, :].rearrange("(p t) r -> p t r", t=t_count),
-                        in_=ov[:, e, :, :],
-                    )
+                if n + 2 == g0 + t_count:
+                    for e in range(E):
+                        nc.sync.dma_start(
+                            out=of[e][g0 * P:(g0 + t_count) * P, :].rearrange("(p t) r -> p t r", t=t_count),
+                            in_=ov[:, e, :, :],
+                        )
 
-        for i in range(NQ + 3):
-            if i < NQ:
-                transpose_quad(i)
-                c = next_chunk[0]
-                if c < len(CHUNKS):
-                    old = c - BIG_BUFS
-                    if chunk_first[old] + CHUNKS[old] == QUAD * (i + 1):
-                        load_chunk(c)
-                        next_chunk[0] = c + 1
-            if 0 <= i - 3 < NQ:
-                out_quad(i - 3)
-            if 0 <= i - 1 < NQ:
-                quantise_quad(i - 1)
-            if 0 <= i - 2 < NQ:
-                mx_quad(i - 2)
+        for i in range(len(RUNS) + 1):
+            if i < len(RUNS):
+                transpose_run(i)
+            if i >= 1:
+                multiply_run(i - 1)

@@ -21,7 +21,7 @@ UNIT = 4
 
 FLOPS = 2 * ROWS * D * COLS
 
-GROUPS = (32, 24, 8)
+GROUPS = (32, 16, 8, 8)
 CHUNKS = (1, 1, 2, 4, 4, 4, 4, 4, 4, 4, 8, 8, 8, 4, 4)
 CHUNK_BUFS = {1: 2, 2: 1, 4: 5, 8: 3}
 RUNS = (2, 2, 4, 8, 8, 8, 8, 8, 8, 4, 2, 2)

@@ -60,7 +60,6 @@ def tile_moelineara_t_kernel(tc, x, W, *outs):
         opool = ctx.enter_context(tc.tile_pool(name="opool", bufs=1))
         psum_t = ctx.enter_context(tc.psum_pool(name="psum_t", bufs=4))
         psum_o = ctx.enter_context(tc.psum_pool(name="psum_o", bufs=4))
-        ctx.enter_context(tc.manual_schedule())
 
         tile_src = {}
         holders = {}

from contextlib import ExitStack

import concourse.mybir as mybir
from concourse.masks import make_identity

F32 = mybir.dt.float32
BF16 = mybir.dt.bfloat16
U32 = mybir.dt.uint32
U8 = mybir.dt.uint8
FP8X4 = mybir.dt.float8_e4m3fn_x4

P = 128
D = 1024
ROWS = 8192
E = 8
R = 32
COLS = E * R
NT = ROWS // P
WORDS = D // 2
UNIT = 4

FLOPS = 2 * ROWS * D * COLS

GROUPS = (32, 16, 8, 8)
CHUNKS = (1, 1, 2, 4, 4, 4, 4, 4, 4, 4, 8, 8, 8, 4, 4)
CHUNK_BUFS = {1: 2, 2: 1, 4: 5, 8: 3}
RUNS = (2, 2, 4, 8, 8, 8, 8, 8, 8, 4, 2, 2)


def tile_moelineara_t_kernel(tc, x, W, *outs):
    nc = tc.nc
    xf = x.flatten_outer_dims()
    wf = W.flatten_outer_dims()
    of = [o.flatten_outer_dims() for o in outs]

    group_of = []
    first = 0
    for s, t_count in enumerate(GROUPS):
        group_of.extend([(s, first, t_count)] * t_count)
        first += t_count
    assert first == NT
    chunk_first = []
    first = 0
    for cnt in CHUNKS:
        chunk_first.append(first)
        first += cnt
    assert first == NT
    run_first = []
    first = 0
    for cnt in RUNS:
        run_first.append(first)
        first += cnt
    assert first == NT

    with ExitStack() as ctx:
        const = ctx.enter_context(tc.tile_pool(name="const", bufs=1))
        xpool = ctx.enter_context(tc.tile_pool(name="xpool", bufs=1))
        gpool = ctx.enter_context(tc.tile_pool(name="gpool", bufs=3))
        qpool = ctx.enter_context(tc.tile_pool(name="qpool", bufs=4))
        opool = ctx.enter_context(tc.tile_pool(name="opool", bufs=1))
        psum_t = ctx.enter_context(tc.psum_pool(name="psum_t", bufs=4))
        psum_o = ctx.enter_context(tc.psum_pool(name="psum_o", bufs=4))

        tile_src = {}
        holders = {}
        state = {"chunk": 0, "transposed": 0}

        def load_chunks():
            while state["chunk"] < len(CHUNKS):
                c = state["chunk"]
                cnt = CHUNKS[c]
                held = holders.get(cnt, [])
                if len(held) >= CHUNK_BUFS[cnt]:
                    old = held[len(held) - CHUNK_BUFS[cnt]]
                    if chunk_first[old] + cnt > state["transposed"]:
                        return
                holders[cnt] = held + [c]
                state["chunk"] = c + 1
                n0 = chunk_first[c]
                s, g0, t_count = group_of[n0]
                xc = xpool.tile([P, cnt * D], BF16, name="x%d" % cnt, tag="x%d" % cnt, bufs=CHUNK_BUFS[cnt])
                rows = xf[g0 * P:(g0 + t_count) * P, :].rearrange("(p t) k -> p t k", t=t_count)
                nc.sync.dma_start(
                    out=xc[:].rearrange("p (t k) -> p t k", k=D),
                    in_=rows[:, n0 - g0:n0 - g0 + cnt, :],
                )
                xw = xc[:].bitcast(F32)
                for j in range(cnt):
                    tile_src[n0 + j] = (xw, j * WORDS)

        def transpose_tile(words_ap, first_word):
            xt = psum_t.tile([P, 4 * P], F32, name="xt")
            for b in range(4):
                nc.tensor.transpose(
                    xt[:, b * P:(b + 1) * P],
                    words_ap[:, first_word + b * P:first_word + (b + 1) * P],
                    ident[:],
                )
            return xt[:].rearrange("p (g u r) -> p g r u", g=2, u=2)

        def copy_on(k, out, in_):
            if k % 2 == 0:
                nc.vector.tensor_copy(out=out, in_=in_)
            else:
                nc.scalar.copy(out=out, in_=in_)

        w_raw = const.tile([P, 2 * D], BF16, name="w_raw")
        nc.sync.dma_start(
            out=w_raw[:].rearrange("p (h k) -> p h k", h=2),
            in_=wf.rearrange("(h p) k -> p h k", p=P),
        )
        load_chunks()

        ident = const.tile([P, P], F32, name="ident")
        make_identity(nc, ident[:])

        w_grouped = const.tile([P, 2 * COLS * 4], BF16, name="w_grouped", align_bytes=64)
        w_words = const.tile([P, 2 * COLS], U32, name="w_words", align_bytes=64)
        w_scales = const.tile([P, 2 * COLS], U8, name="w_scales", align_bytes=64)
        wg = w_grouped[:].bitcast(F32).rearrange("p (g c u) -> p g c u", g=2, u=2)
        for h in range(2):
            copy_on(h, wg[:, :, h * P:(h + 1) * P, :], transpose_tile(w_raw[:].bitcast(F32), h * WORDS))
        nc.vector.quantize_mx(out=w_words[:].bitcast(FP8X4), scales=w_scales[:], in_=w_grouped[:])

        quant = {}
        out_sb = {}

        def transpose_run(i):
            n0 = run_first[i]
            units = []
            for u0 in range(n0, n0 + RUNS[i], UNIT):
                cnt = min(UNIT, n0 + RUNS[i] - u0)
                gt = gpool.tile([P, cnt * D], BF16, name="grouped", align_bytes=64)
                gf = gt[:].bitcast(F32)
                for j in range(cnt):
                    xw, off = tile_src[u0 + j]
                    copy_on(
                        u0 + j,
                        gf[:, j * WORDS:(j + 1) * WORDS].rearrange("p (g r u) -> p g r u", g=2, u=2),
                        transpose_tile(xw, off),
                    )
                units.append((u0, cnt, gt))
            state["transposed"] = n0 + RUNS[i]
            load_chunks()
            for u0, cnt, gt in units:
                words = qpool.tile([P, cnt * 2 * P], U32, name="words", align_bytes=64)
                scales = qpool.tile([P, cnt * 2 * P], U8, name="scales", align_bytes=64)
                nc.vector.quantize_mx(out=words[:].bitcast(FP8X4), scales=scales[:], in_=gt[:])
                for j in range(cnt):
                    quant[u0 + j] = (words, scales, j * 2 * P)

        def multiply_run(i):
            for n in range(run_first[i], run_first[i] + RUNS[i], 2):
                acc = psum_o.tile([P, 2 * COLS], F32, name="acc")
                for jj in range(2):
                    words, scales, c0 = quant[n + jj]
                    for g in range(2):
                        nc.tensor.matmul_mx(
                            out=acc[:, jj * COLS:(jj + 1) * COLS],
                            lhsT=words[:, c0 + g * P:c0 + (g + 1) * P].bitcast(FP8X4),
                            lhsT_scale=scales[:, c0 + g * P:c0 + (g + 1) * P],
                            rhs=w_words[:, g * COLS:(g + 1) * COLS].bitcast(FP8X4),
                            rhs_scale=w_scales[:, g * COLS:(g + 1) * COLS],
                            start=(g == 0),
                            stop=(g == 1),
                        )
                s, g0, t_count = group_of[n]
                if n == g0:
                    out_sb[s] = opool.tile([P, E * t_count * R], F32, name="out%d" % s, tag="out%d" % s)
                ov = out_sb[s][:].rearrange("p (e t r) -> p e t r", e=E, r=R)
                nc.scalar.copy(
                    out=ov[:, :, n - g0:n - g0 + 2, :],
                    in_=acc[:].rearrange("p (t e r) -> p e t r", t=2, r=R),
                )
                if n + 2 == g0 + t_count:
                    for e in range(E):
                        nc.sync.dma_start(
                            out=of[e][g0 * P:(g0 + t_count) * P, :].rearrange("(p t) r -> p t r", t=t_count),
                            in_=ov[:, e, :, :],
                        )

        for i in range(len(RUNS) + 1):
            if i < len(RUNS):
                transpose_run(i)
            if i >= 1:
                multiply_run(i - 1)
